import numpy as np
import ml_dtypes


def mxq(x, axis, fmt="e4m3"):
    dtype, down = {"e4m3": (ml_dtypes.float8_e4m3fn, 7), "e5m2": (ml_dtypes.float8_e5m2, 14)}[fmt]
    v = np.moveaxis(np.asarray(x, np.float32).astype(ml_dtypes.bfloat16).astype(np.float64), axis, -1)
    blocks = v.reshape(v.shape[:-1] + (-1, 32))
    amax = np.abs(blocks).max(-1, keepdims=True)
    byte = np.maximum(np.where(amax > 0, np.frexp(amax)[1] - 1 + 127, 0) - down, 1)
    scale = np.exp2(byte - 127.0)
    codes = (blocks / scale).astype(np.float32).astype(dtype).astype(np.float64)
    return np.moveaxis((codes * scale).reshape(v.shape), -1, axis)


WIDE = False


def mx_kscale(k):
    if not WIDE:
        return np.ones(k)
    levels = np.array([10, -10, 5, -5, 0])
    a = np.random.permutation(np.resize(levels, k // 512 * 4)).reshape(k // 512, 4)
    idx = np.arange(k)
    return np.exp2(a[idx // 512, idx % 128 // 32])


BF16 = ml_dtypes.bfloat16


def bf(x):
    return np.asarray(x, np.float32).astype(BF16)


def f64(x):
    return np.asarray(x).astype(np.float64)


B, N, C, DIM, H = 4, 128, 2048, 2048, 16
D = DIM // H // 2
LAYER_NUM = 12
LAM_INIT = 0.8 - 0.6 * np.exp(-0.3 * LAYER_NUM)
SCALE = D ** -0.5


def split_qk(y):
    y = y.reshape(B, N, H, D, 2)
    return np.moveaxis(y, -1, 2).reshape(B, N, 2 * H, D)


def setup_inputs():
    s = mx_kscale(C)
    ls = 0.45 / D ** 0.25
    return {"x": bf(np.random.standard_normal((B, N, C)) * s),
            "Wq": bf(np.random.standard_normal((DIM, C)) / np.sqrt(C) / s),
            "Wk": bf(np.random.standard_normal((DIM, C)) / np.sqrt(C) / s),
            "lq1": bf(np.random.standard_normal(D) * ls),
            "lq2": bf(np.random.standard_normal(D) * ls),
            "lk1": bf(np.random.standard_normal(D) * ls),
            "lk2": bf(np.random.standard_normal(D) * ls)}


def reference(x, Wq, Wk, lq1, lq2, lk1, lk2):
    xq = mxq(f64(x), 2, "e4m3")
    q = split_qk(xq @ mxq(f64(Wq), 1, "e4m3").T) * SCALE
    k = split_qk(xq @ mxq(f64(Wk), 1, "e4m3").T)
    sc = np.stack([(q[:, :, i:i + 1, :] * k).sum(-1) for i in range(2 * H)], axis=2)
    e = np.exp(sc - sc.max(-1, keepdims=True))
    att = e / e.sum(-1, keepdims=True)
    lam = np.exp(np.sum(f64(lq1) * f64(lk1))) - np.exp(np.sum(f64(lq2) * f64(lk2))) + LAM_INIT
    return att[:, :, :H, :H] - lam * att[:, :, H:, H:]

@@ -1,0 +1,249 @@
+import math
+
+import concourse.mybir as mybir
+from concourse.masks import make_identity
+
+F32 = mybir.dt.float32
+BF16 = mybir.dt.bfloat16
+U32 = mybir.dt.uint32
+U8 = mybir.dt.uint8
+FP8X4 = mybir.dt.float8_e4m3fn_x4
+ALU = mybir.AluOpType
+ACT = mybir.ActivationFunctionType
+AXIS_X = mybir.AxisListType.X
+
+P = 128
+PACK = 4
+K_PASS = P * PACK
+TOKENS = 512
+C = 2048
+DIM = 2048
+H = 16
+D = 64
+HEAD_ROWS = 2 * H
+PASSES = C // K_PASS
+CHUNK = 512
+ROW_TILES = CHUNK // P
+CHUNKS_PER_W = DIM // CHUNK
+HEADS_PER_CHUNK = CHUNK // (2 * D)
+WORDS = P
+SLOTS = TOKENS // 2
+GROUPS = SLOTS // 2
+GROUPS_PER_BANK = 8
+BATCH = 16
+BATCHES = GROUPS // BATCH
+LAG = 2
+SCALE = D ** -0.5
+LAM_INIT = 0.8 - 0.6 * math.exp(-0.3 * 12)
+
+FLOPS = 2 * TOKENS * C * DIM * 2 + 2 * TOKENS * HEAD_ROWS * HEAD_ROWS * D
+
+
+def tile_differentialattention_pa_kernel(tc, x, Wq, Wk, lq1, lq2, lk1, lk2, out):
+    nc = tc.nc
+
+    x_rows = x.rearrange("b n c -> (b n) c").rearrange("(pr r t) c -> pr r t c", pr=2, t=2)
+    out_rows = out.rearrange("b n a h -> (b n a) h").rearrange("(w r) h -> r w h", r=4 * H)
+
+    with tc.tile_pool(name="const", bufs=1) as const, tc.tile_pool(name="heads", bufs=1) as heads, tc.psum_pool(
+        name="turned", bufs=4
+    ) as turned, tc.psum_pool(name="sums", bufs=4) as sums:
+        ident = const.tile([P, P], F32)
+        make_identity(nc, ident[:])
+
+        q_cols = heads.tile([P, SLOTS, 2 * HEAD_ROWS], F32)
+        k_cols = heads.tile([P, SLOTS, HEAD_ROWS], F32)
+        for piece in range(16):
+            nc.gpsimd.memset(q_cols[:, 16 * piece : 16 * piece + 16, :], 0.0)
+
+        select = const.tile([P, 2, P], F32)
+        nc.vector.memset(select[:], 0.0)
+        ident_rows = ident[:].rearrange("p (u j r) -> p u j r", u=2, j=2)
+        for j in range(2):
+            nc.vector.tensor_copy(
+                out=select[:, j, 0 : 4 * H].rearrange("p (u r) -> p u r", u=2), in_=ident_rows[:, :, j, :]
+            )
+
+        with tc.tile_pool(name="raw", bufs=3) as raw_pool, tc.tile_pool(name="grouped", bufs=2) as grouped_pool, tc.tile_pool(
+            name="wq", bufs=2
+        ) as w_pool, tc.tile_pool(name="xq", bufs=1) as x_pool, tc.tile_pool(name="y", bufs=2) as y_pool:
+
+            def turn_rows(raw):
+                grouped = grouped_pool.tile([P, PASSES, PACK * CHUNK], BF16, align_bytes=64)
+                raw_words = raw[:].bitcast(F32)
+                grouped_words = grouped[:].bitcast(F32).rearrange("p g (o u) -> p g o u", u=2)
+                for r in range(ROW_TILES):
+                    for pair in range(PASSES // 2):
+                        bank = turned.tile([P, 2, 2, P], F32, tag="turned")
+                        for g in range(2):
+                            for u in range(2):
+                                first = 2 * WORDS * (2 * pair + g) + WORDS * u
+                                nc.tensor.transpose(
+                                    out=bank[:, g, u, :],
+                                    in_=raw_words[:, r, first : first + WORDS],
+                                    identity=ident[:],
+                                )
+                        copy = nc.scalar.copy if pair == 0 else nc.vector.tensor_copy
+                        copy(
+                            out=grouped_words[:, 2 * pair : 2 * pair + 2, P * r : P * r + P, :],
+                            in_=bank[:].rearrange("p g u o -> p g o u"),
+                        )
+                return grouped
+
+            def quantise(grouped, codes, scales):
+                for g in range(PASSES):
+                    nc.vector.quantize_mx(
+                        out=codes[:, g, :].bitcast(FP8X4), scales=scales[:, g, :], in_=grouped[:, g, :]
+                    )
+
+            def project(w_codes, w_scales):
+                y = y_pool.tile([P, 2, HEADS_PER_CHUNK, ROW_TILES, D], F32)
+                for t in range(ROW_TILES):
+                    tokens = slice(P * t, P * t + P)
+                    acc = sums.tile([P, CHUNK], F32, tag="sums")
+                    for g in range(PASSES):
+                        nc.tensor.matmul_mx(
+                            out=acc[:],
+                            lhsT=x_codes[:, g, tokens].bitcast(FP8X4),
+                            lhsT_scale=x_scales[:, g, tokens],
+                            rhs=w_codes[:, g, :].bitcast(FP8X4),
+                            rhs_scale=w_scales[:, g, :],
+                            start=(g == 0),
+                            stop=(g == PASSES - 1),
+                        )
+                    nc.scalar.copy(
+                        out=y[:, :, :, t, :], in_=acc[:].rearrange("p (h d j) -> p j h d", h=HEADS_PER_CHUNK, j=2)
+                    )
+                return y
+
+            def turn_heads(y, is_q, first_head):
+                for j in range(2):
+                    for pr in range(2):
+                        bank = turned.tile([P, HEADS_PER_CHUNK, P], F32, tag="turned")
+                        for h in range(HEADS_PER_CHUNK):
+                            nc.tensor.transpose(
+                                out=bank[:, h, :],
+                                in_=y[:, j, h, 2 * pr : 2 * pr + 2, :].rearrange("p t d -> p (t d)"),
+                                identity=ident[:],
+                            )
+                        by_slot = bank[:].rearrange("p h s -> p s h")
+                        slots = slice(P * pr, P * pr + P)
+                        copy = nc.scalar.copy if pr == 0 else nc.vector.tensor_copy
+                        if is_q:
+                            for t in range(2):
+                                rows = slice(D * t, D * t + D)
+                                col = 2 * H * j + H * t + first_head
+                                copy(out=q_cols[rows, slots, col : col + HEADS_PER_CHUNK], in_=by_slot[rows])
+                        else:
+                            col = H * j + first_head
+                            copy(out=k_cols[:, slots, col : col + HEADS_PER_CHUNK], in_=by_slot)
+
+            def load_w(c):
+                w = Wk if c < CHUNKS_PER_W else Wq
+                first = CHUNK * (c % CHUNKS_PER_W)
+                raw = raw_pool.tile([P, ROW_TILES, C], BF16, tag="raw")
+                for r in range(ROW_TILES):
+                    nc.sync.dma_start(out=raw[:, r, :], in_=w[first + P * r : first + P * r + P, :])
+                return raw
+
+            def new_w_codes():
+                codes = w_pool.tile([P, PASSES, CHUNK], U32, align_bytes=64, tag="w_codes")
+                scales = w_pool.tile([P, PASSES, CHUNK], U8, align_bytes=64, tag="w_scales")
+                return codes, scales
+
+            n_chunks = 2 * CHUNKS_PER_W
+            x_raw = raw_pool.tile([P, ROW_TILES, C], BF16, tag="raw")
+            for pr in range(2):
+                nc.sync.dma_start(out=x_raw[:, 2 * pr : 2 * pr + 2, :], in_=x_rows[pr])
+            raws = {0: load_w(0), 1: load_w(1)}
+
+            x_codes = x_pool.tile([P, PASSES, TOKENS], U32, align_bytes=64)
+            x_scales = x_pool.tile([P, PASSES, TOKENS], U8, align_bytes=64)
+            quantise(turn_rows(x_raw), x_codes, x_scales)
+
+            ready = {0: new_w_codes()}
+            quantise(turn_rows(raws[0]), ready[0][0], ready[0][1])
+
+            ys = {}
+            for c in range(n_chunks):
+                if c + 2 < n_chunks:
+                    raws[c + 2] = load_w(c + 2)
+                if c + 1 < n_chunks:
+                    grouped_next = turn_rows(raws[c + 1])
+                if c >= 1:
+                    turn_heads(ys[c - 1], c - 1 >= CHUNKS_PER_W, HEADS_PER_CHUNK * ((c - 1) % CHUNKS_PER_W))
+                if c + 1 < n_chunks:
+                    ready[c + 1] = new_w_codes()
+                    quantise(grouped_next, ready[c + 1][0], ready[c + 1][1])
+                ys[c] = project(ready[c][0], ready[c][1])
+            turn_heads(ys[n_chunks - 1], True, HEADS_PER_CHUNK * (CHUNKS_PER_W - 1))
+
+        vectors = const.tile([P, 4, D], BF16)
+        for i, vec in enumerate((lq1, lq2, lk1, lk2)):
+            nc.sync.dma_start(out=vectors[:, i, :], in_=vec.partition_broadcast(P))
+        products = const.tile([P, 2, D], F32)
+        nc.vector.tensor_tensor(out=products[:], in0=vectors[:, 0:2, :], in1=vectors[:, 2:4, :], op=ALU.mult)
+        dots = const.tile([P, 2], F32)
+        nc.vector.tensor_reduce(out=dots[:], in_=products[:], axis=AXIS_X, op=ALU.add)
+        exps = const.tile([P, 2], F32)
+        nc.scalar.activation(out=exps[:], in_=dots[:], func=ACT.Exp)
+        neg_lam = const.tile([P, 1], F32)
+        nc.vector.tensor_scalar(
+            out=neg_lam[:], in0=exps[:, 1:2], scalar1=exps[:, 0:1], scalar2=-LAM_INIT, op0=ALU.subtract, op1=ALU.add
+        )
+        nc.vector.tensor_scalar(
+            out=select[:, 1, :], in0=select[:, 1, :], scalar1=neg_lam[:, 0:1], scalar2=None, op0=ALU.mult
+        )
+
+        with tc.tile_pool(name="soft", bufs=LAG + 2) as soft, tc.tile_pool(name="stats", bufs=LAG + 2) as stats:
+
+            def scores(b):
+                att = soft.tile([P, BATCH, HEAD_ROWS], F32, tag="att")
+                for half in range(BATCH // GROUPS_PER_BANK):
+                    bank = sums.tile([P, GROUPS_PER_BANK, 2 * HEAD_ROWS], F32, tag="sums")
+                    for i in range(GROUPS_PER_BANK):
+                        w = BATCH * b + GROUPS_PER_BANK * half + i
+                        nc.tensor.matmul(
+                            out=bank[:, i, :],
+                            lhsT=q_cols[:, 2 * w : 2 * w + 2, :].rearrange("p s c -> p (s c)"),
+                            rhs=k_cols[:, 2 * w : 2 * w + 2, :].rearrange("p s c -> p (s c)"),
+                            start=True,
+                            stop=True,
+                        )
+                    for u in range(2):
+                        rows = slice(D * u, D * u + D)
+                        nc.scalar.copy(
+                            out=att[rows, GROUPS_PER_BANK * half : GROUPS_PER_BANK * (half + 1), :],
+                            in_=bank[rows, :, HEAD_ROWS * u : HEAD_ROWS * (u + 1)],
+                        )
+                return att
+
+            def softmax(att):
+                wide = [P, BATCH, HEAD_ROWS]
+                top = stats.tile([P, BATCH], F32, tag="top")
+                nc.vector.tensor_reduce(out=top[:], in_=att[:], axis=AXIS_X, op=ALU.max)
+                nc.vector.tensor_tensor(out=att[:], in0=att[:], in1=top[:].unsqueeze(2).to_broadcast(wide), op=ALU.subtract)
+                nc.scalar.activation(out=att[:], in_=att[:], func=ACT.Exp, scale=SCALE)
+                total = stats.tile([P, BATCH], F32, tag="total")
+                nc.vector.tensor_reduce(out=total[:], in_=att[:], axis=AXIS_X, op=ALU.add)
+                inverse = stats.tile([P, BATCH], F32, tag="inverse")
+                nc.vector.reciprocal(out=inverse[:], in_=total[:])
+                nc.vector.tensor_tensor(out=att[:], in0=att[:], in1=inverse[:].unsqueeze(2).to_broadcast(wide), op=ALU.mult)
+
+            def combine(b, att):
+                diff = turned.tile([P, BATCH, H], F32, tag="turned")
+                for j in range(2):
+                    nc.tensor.matmul(
+                        out=diff[:], lhsT=select[:, j, :], rhs=att[:, :, H * j : H * j + H], start=(j == 0), stop=(j == 1)
+                    )
+                result = soft.tile([4 * H, BATCH, H], F32, tag="result")
+                nc.scalar.copy(out=result[:], in_=diff[0 : 4 * H])
+                nc.sync.dma_start(out=out_rows[:, BATCH * b : BATCH * (b + 1), :], in_=result[:])
+
+            atts = {}
+            for b in range(BATCHES + LAG):
+                if b < BATCHES:
+                    atts[b] = scores(b)
+                    softmax(atts[b])
+                if b >= LAG:
+                    combine(b - LAG, atts[b - LAG])

@@ -32,7 +32,6 @@ GROUPS = SLOTS // 2
 GROUPS_PER_BANK = 8
 BATCH = 16
 BATCHES = GROUPS // BATCH
-LAG = 2
 SCALE = D ** -0.5
 LAM_INIT = 0.8 - 0.6 * math.exp(-0.3 * 12)
 
@@ -45,9 +44,9 @@ def tile_differentialattention_pa_kernel(tc, x, Wq, Wk, lq1, lq2, lk1, lk2, out)
     x_rows = x.rearrange("b n c -> (b n) c").rearrange("(pr r t) c -> pr r t c", pr=2, t=2)
     out_rows = out.rearrange("b n a h -> (b n a) h").rearrange("(w r) h -> r w h", r=4 * H)
 
-    with tc.tile_pool(name="const", bufs=1) as const, tc.tile_pool(name="heads", bufs=1) as heads, tc.psum_pool(
-        name="turned", bufs=4
-    ) as turned, tc.psum_pool(name="sums", bufs=4) as sums:
+    with tc.manual_schedule(), tc.tile_pool(name="const", bufs=1) as const, tc.tile_pool(
+        name="heads", bufs=1
+    ) as heads, tc.psum_pool(name="turned", bufs=4) as turned, tc.psum_pool(name="sums", bufs=4) as sums:
         ident = const.tile([P, P], F32)
         make_identity(nc, ident[:])
 
@@ -64,31 +63,47 @@ def tile_differentialattention_pa_kernel(tc, x, Wq, Wk, lq1, lq2, lk1, lk2, out)
                 out=select[:, j, 0 : 4 * H].rearrange("p (u r) -> p u r", u=2), in_=ident_rows[:, :, j, :]
             )
 
+        vectors = const.tile([P, 4, D], BF16)
+        for i, vec in enumerate((lq1, lq2, lk1, lk2)):
+            nc.scalar.dma_start(out=vectors[:, i, :], in_=vec.partition_broadcast(P))
+        products = const.tile([P, 2, D], F32)
+        nc.vector.tensor_tensor(out=products[:], in0=vectors[:, 0:2, :], in1=vectors[:, 2:4, :], op=ALU.mult)
+        dots = const.tile([P, 2], F32)
+        nc.vector.tensor_reduce(out=dots[:], in_=products[:], axis=AXIS_X, op=ALU.add)
+        exps = const.tile([P, 2], F32)
+        nc.scalar.activation(out=exps[:], in_=dots[:], func=ACT.Exp)
+        neg_lam = const.tile([P, 1], F32)
+        nc.vector.tensor_scalar(
+            out=neg_lam[:], in0=exps[:, 1:2], scalar1=exps[:, 0:1], scalar2=-LAM_INIT, op0=ALU.subtract, op1=ALU.add
+        )
+        nc.vector.tensor_scalar(
+            out=select[:, 1, :], in0=select[:, 1, :], scalar1=neg_lam[:, 0:1], scalar2=None, op0=ALU.mult
+        )
+
         with tc.tile_pool(name="raw", bufs=3) as raw_pool, tc.tile_pool(name="grouped", bufs=2) as grouped_pool, tc.tile_pool(
             name="wq", bufs=2
         ) as w_pool, tc.tile_pool(name="xq", bufs=1) as x_pool, tc.tile_pool(name="y", bufs=2) as y_pool:
 
-            def turn_rows(raw):
+            def new_grouped():
                 grouped = grouped_pool.tile([P, PASSES, PACK * CHUNK], BF16, align_bytes=64)
+                return grouped
+
+            def turn_row_tile(raw, grouped, r):
                 raw_words = raw[:].bitcast(F32)
                 grouped_words = grouped[:].bitcast(F32).rearrange("p g (o u) -> p g o u", u=2)
-                for r in range(ROW_TILES):
-                    for pair in range(PASSES // 2):
-                        bank = turned.tile([P, 2, 2, P], F32, tag="turned")
-                        for g in range(2):
-                            for u in range(2):
-                                first = 2 * WORDS * (2 * pair + g) + WORDS * u
-                                nc.tensor.transpose(
-                                    out=bank[:, g, u, :],
-                                    in_=raw_words[:, r, first : first + WORDS],
-                                    identity=ident[:],
-                                )
-                        copy = nc.scalar.copy if pair == 0 else nc.vector.tensor_copy
-                        copy(
-                            out=grouped_words[:, 2 * pair : 2 * pair + 2, P * r : P * r + P, :],
-                            in_=bank[:].rearrange("p g u o -> p g o u"),
-                        )
-                return grouped
+                for pair in range(PASSES // 2):
+                    bank = turned.tile([P, 2, 2, P], F32, tag="turned")
+                    for g in range(2):
+                        for u in range(2):
+                            first = 2 * WORDS * (2 * pair + g) + WORDS * u
+                            nc.tensor.transpose(
+                                out=bank[:, g, u, :], in_=raw_words[:, r, first : first + WORDS], identity=ident[:]
+                            )
+                    copy = nc.scalar.copy if pair == 0 else nc.vector.tensor_copy
+                    copy(
+                        out=grouped_words[:, 2 * pair : 2 * pair + 2, P * r : P * r + P, :],
+                        in_=bank[:].rearrange("p g u o -> p g o u"),
+                    )
 
             def quantise(grouped, codes, scales):
                 for g in range(PASSES):
@@ -96,47 +111,43 @@ def tile_differentialattention_pa_kernel(tc, x, Wq, Wk, lq1, lq2, lk1, lk2, out)
                         out=codes[:, g, :].bitcast(FP8X4), scales=scales[:, g, :], in_=grouped[:, g, :]
                     )
 
-            def project(w_codes, w_scales):
-                y = y_pool.tile([P, 2, HEADS_PER_CHUNK, ROW_TILES, D], F32)
-                for t in range(ROW_TILES):
-                    tokens = slice(P * t, P * t + P)
-                    acc = sums.tile([P, CHUNK], F32, tag="sums")
-                    for g in range(PASSES):
-                        nc.tensor.matmul_mx(
-                            out=acc[:],
-                            lhsT=x_codes[:, g, tokens].bitcast(FP8X4),
-                            lhsT_scale=x_scales[:, g, tokens],
-                            rhs=w_codes[:, g, :].bitcast(FP8X4),
-                            rhs_scale=w_scales[:, g, :],
-                            start=(g == 0),
-                            stop=(g == PASSES - 1),
-                        )
-                    nc.scalar.copy(
-                        out=y[:, :, :, t, :], in_=acc[:].rearrange("p (h d j) -> p j h d", h=HEADS_PER_CHUNK, j=2)
+            def project_tile(w_codes, w_scales, y, t):
+                tokens = slice(P * t, P * t + P)
+                acc = sums.tile([P, CHUNK], F32, tag="sums")
+                for g in range(PASSES):
+                    nc.tensor.matmul_mx(
+                        out=acc[:],
+                        lhsT=x_codes[:, g, tokens].bitcast(FP8X4),
+                        lhsT_scale=x_scales[:, g, tokens],
+                        rhs=w_codes[:, g, :].bitcast(FP8X4),
+                        rhs_scale=w_scales[:, g, :],
+                        start=(g == 0),
+                        stop=(g == PASSES - 1),
                     )
-                return y
+                nc.scalar.copy(
+                    out=y[:, :, :, t, :], in_=acc[:].rearrange("p (h d j) -> p j h d", h=HEADS_PER_CHUNK, j=2)
+                )
 
-            def turn_heads(y, is_q, first_head):
-                for j in range(2):
-                    for pr in range(2):
-                        bank = turned.tile([P, HEADS_PER_CHUNK, P], F32, tag="turned")
-                        for h in range(HEADS_PER_CHUNK):
-                            nc.tensor.transpose(
-                                out=bank[:, h, :],
-                                in_=y[:, j, h, 2 * pr : 2 * pr + 2, :].rearrange("p t d -> p (t d)"),
-                                identity=ident[:],
-                            )
-                        by_slot = bank[:].rearrange("p h s -> p s h")
-                        slots = slice(P * pr, P * pr + P)
-                        copy = nc.scalar.copy if pr == 0 else nc.vector.tensor_copy
-                        if is_q:
-                            for t in range(2):
-                                rows = slice(D * t, D * t + D)
-                                col = 2 * H * j + H * t + first_head
-                                copy(out=q_cols[rows, slots, col : col + HEADS_PER_CHUNK], in_=by_slot[rows])
-                        else:
-                            col = H * j + first_head
-                            copy(out=k_cols[:, slots, col : col + HEADS_PER_CHUNK], in_=by_slot)
+            def turn_heads(y, n, is_q, first_head):
+                pr, j = n // 2, n % 2
+                bank = turned.tile([P, HEADS_PER_CHUNK, P], F32, tag="turned")
+                for h in range(HEADS_PER_CHUNK):
+                    nc.tensor.transpose(
+                        out=bank[:, h, :],
+                        in_=y[:, j, h, 2 * pr : 2 * pr + 2, :].rearrange("p t d -> p (t d)"),
+                        identity=ident[:],
+                    )
+                by_slot = bank[:].rearrange("p h s -> p s h")
+                slots = slice(P * pr, P * pr + P)
+                copy = nc.vector.tensor_copy if n % 2 == 0 else nc.scalar.copy
+                if is_q:
+                    for t in range(2):
+                        rows = slice(D * t, D * t + D)
+                        col = 2 * H * j + H * t + first_head
+                        copy(out=q_cols[rows, slots, col : col + HEADS_PER_CHUNK], in_=by_slot[rows])
+                else:
+                    col = H * j + first_head
+                    copy(out=k_cols[:, slots, col : col + HEADS_PER_CHUNK], in_=by_slot)
 
             def load_w(c):
                 w = Wk if c < CHUNKS_PER_W else Wq
@@ -159,46 +170,42 @@ def tile_differentialattention_pa_kernel(tc, x, Wq, Wk, lq1, lq2, lk1, lk2, out)
 
             x_codes = x_pool.tile([P, PASSES, TOKENS], U32, align_bytes=64)
             x_scales = x_pool.tile([P, PASSES, TOKENS], U8, align_bytes=64)
-            quantise(turn_rows(x_raw), x_codes, x_scales)
+            x_grouped = new_grouped()
+            for r in range(ROW_TILES):
+                turn_row_tile(x_raw, x_grouped, r)
+            quantise(x_grouped, x_codes, x_scales)
 
+            groupeds = {0: new_grouped()}
+            for r in range(ROW_TILES):
+                turn_row_tile(raws[0], groupeds[0], r)
             ready = {0: new_w_codes()}
-            quantise(turn_rows(raws[0]), ready[0][0], ready[0][1])
+            quantise(groupeds[0], ready[0][0], ready[0][1])
 
             ys = {}
             for c in range(n_chunks):
                 if c + 2 < n_chunks:
                     raws[c + 2] = load_w(c + 2)
                 if c + 1 < n_chunks:
-                    grouped_next = turn_rows(raws[c + 1])
-                if c >= 1:
-                    turn_heads(ys[c - 1], c - 1 >= CHUNKS_PER_W, HEADS_PER_CHUNK * ((c - 1) % CHUNKS_PER_W))
+                    groupeds[c + 1] = new_grouped()
+                ys[c] = y_pool.tile([P, 2, HEADS_PER_CHUNK, ROW_TILES, D], F32, tag="y", name="y")
+                for t in range(ROW_TILES):
+                    if c + 1 < n_chunks:
+                        turn_row_tile(raws[c + 1], groupeds[c + 1], t)
+                    if c >= 1:
+                        turn_heads(ys[c - 1], t, c - 1 >= CHUNKS_PER_W, HEADS_PER_CHUNK * ((c - 1) % CHUNKS_PER_W))
+                    project_tile(ready[c][0], ready[c][1], ys[c], t)
                 if c + 1 < n_chunks:
                     ready[c + 1] = new_w_codes()
-                    quantise(grouped_next, ready[c + 1][0], ready[c + 1][1])
-                ys[c] = project(ready[c][0], ready[c][1])
-            turn_heads(ys[n_chunks - 1], True, HEADS_PER_CHUNK * (CHUNKS_PER_W - 1))
+                    quantise(groupeds[c + 1], ready[c + 1][0], ready[c + 1][1])
+            for n in range(4):
+                turn_heads(ys[n_chunks - 1], n, True, HEADS_PER_CHUNK * (CHUNKS_PER_W - 1))
 
-        vectors = const.tile([P, 4, D], BF16)
-        for i, vec in enumerate((lq1, lq2, lk1, lk2)):
-            nc.sync.dma_start(out=vectors[:, i, :], in_=vec.partition_broadcast(P))
-        products = const.tile([P, 2, D], F32)
-        nc.vector.tensor_tensor(out=products[:], in0=vectors[:, 0:2, :], in1=vectors[:, 2:4, :], op=ALU.mult)
-        dots = const.tile([P, 2], F32)
-        nc.vector.tensor_reduce(out=dots[:], in_=products[:], axis=AXIS_X, op=ALU.add)
-        exps = const.tile([P, 2], F32)
-        nc.scalar.activation(out=exps[:], in_=dots[:], func=ACT.Exp)
-        neg_lam = const.tile([P, 1], F32)
-        nc.vector.tensor_scalar(
-            out=neg_lam[:], in0=exps[:, 1:2], scalar1=exps[:, 0:1], scalar2=-LAM_INIT, op0=ALU.subtract, op1=ALU.add
-        )
-        nc.vector.tensor_scalar(
-            out=select[:, 1, :], in0=select[:, 1, :], scalar1=neg_lam[:, 0:1], scalar2=None, op0=ALU.mult
-        )
-
-        with tc.tile_pool(name="soft", bufs=LAG + 2) as soft, tc.tile_pool(name="stats", bufs=LAG + 2) as stats:
+        with tc.tile_pool(name="soft", bufs=4) as soft, tc.tile_pool(name="stats", bufs=4) as stats:
+            wide = [P, BATCH, HEAD_ROWS]
+            atts, tops, totals = {}, {}, {}
 
             def scores(b):
-                att = soft.tile([P, BATCH, HEAD_ROWS], F32, tag="att")
+                atts[b] = soft.tile(wide, F32, tag="att", name="att")
                 for half in range(BATCH // GROUPS_PER_BANK):
                     bank = sums.tile([P, GROUPS_PER_BANK, 2 * HEAD_ROWS], F32, tag="sums")
                     for i in range(GROUPS_PER_BANK):
@@ -213,37 +220,52 @@ def tile_differentialattention_pa_kernel(tc, x, Wq, Wk, lq1, lq2, lk1, lk2, out)
                     for u in range(2):
                         rows = slice(D * u, D * u + D)
                         nc.scalar.copy(
-                            out=att[rows, GROUPS_PER_BANK * half : GROUPS_PER_BANK * (half + 1), :],
+                            out=atts[b][rows, GROUPS_PER_BANK * half : GROUPS_PER_BANK * (half + 1), :],
                             in_=bank[rows, :, HEAD_ROWS * u : HEAD_ROWS * (u + 1)],
                         )
-                return att
 
-            def softmax(att):
-                wide = [P, BATCH, HEAD_ROWS]
-                top = stats.tile([P, BATCH], F32, tag="top")
-                nc.vector.tensor_reduce(out=top[:], in_=att[:], axis=AXIS_X, op=ALU.max)
-                nc.vector.tensor_tensor(out=att[:], in0=att[:], in1=top[:].unsqueeze(2).to_broadcast(wide), op=ALU.subtract)
+            def largest(b):
+                tops[b] = stats.tile([P, BATCH], F32, tag="top", name="top")
+                nc.vector.tensor_reduce(out=tops[b][:], in_=atts[b][:], axis=AXIS_X, op=ALU.max)
+
+            def shift_and_exp(b):
+                att = atts[b]
+                nc.vector.tensor_tensor(
+                    out=att[:], in0=att[:], in1=tops[b][:].unsqueeze(2).to_broadcast(wide), op=ALU.subtract
+                )
                 nc.scalar.activation(out=att[:], in_=att[:], func=ACT.Exp, scale=SCALE)
-                total = stats.tile([P, BATCH], F32, tag="total")
-                nc.vector.tensor_reduce(out=total[:], in_=att[:], axis=AXIS_X, op=ALU.add)
-                inverse = stats.tile([P, BATCH], F32, tag="inverse")
-                nc.vector.reciprocal(out=inverse[:], in_=total[:])
-                nc.vector.tensor_tensor(out=att[:], in0=att[:], in1=inverse[:].unsqueeze(2).to_broadcast(wide), op=ALU.mult)
 
-            def combine(b, att):
+            def add_up(b):
+                totals[b] = stats.tile([P, BATCH], F32, tag="total", name="total")
+                nc.vector.tensor_reduce(out=totals[b][:], in_=atts[b][:], axis=AXIS_X, op=ALU.add)
+
+            def normalise(b):
+                att = atts[b]
+                inverse = stats.tile([P, BATCH], F32, tag="inverse")
+                nc.vector.reciprocal(out=inverse[:], in_=totals[b][:])
+                nc.vector.tensor_tensor(
+                    out=att[:], in0=att[:], in1=inverse[:].unsqueeze(2).to_broadcast(wide), op=ALU.mult
+                )
+
+            def combine(b):
                 diff = turned.tile([P, BATCH, H], F32, tag="turned")
                 for j in range(2):
                     nc.tensor.matmul(
-                        out=diff[:], lhsT=select[:, j, :], rhs=att[:, :, H * j : H * j + H], start=(j == 0), stop=(j == 1)
+                        out=diff[:], lhsT=select[:, j, :], rhs=atts[b][:, :, H * j : H * j + H], start=(j == 0), stop=(j == 1)
                     )
                 result = soft.tile([4 * H, BATCH, H], F32, tag="result")
                 nc.scalar.copy(out=result[:], in_=diff[0 : 4 * H])
                 nc.sync.dma_start(out=out_rows[:, BATCH * b : BATCH * (b + 1), :], in_=result[:])
 
-            atts = {}
-            for b in range(BATCHES + LAG):
+            for b in range(BATCHES + 2):
                 if b < BATCHES:
-                    atts[b] = scores(b)
-                    softmax(atts[b])
-                if b >= LAG:
-                    combine(b - LAG, atts[b - LAG])
+                    scores(b)
+                    largest(b)
+                if 1 <= b <= BATCHES:
+                    add_up(b - 1)
+                if b < BATCHES:
+                    shift_and_exp(b)
+                if 1 <= b <= BATCHES:
+                    normalise(b - 1)
+                if b >= 2:
+                    combine(b - 2)

@@ -29,9 +29,9 @@ HEADS_PER_CHUNK = CHUNK // (2 * D)
 WORDS = P
 SLOTS = TOKENS // 2
 GROUPS = SLOTS // 2
-GROUPS_PER_BANK = 8
-BATCH = 16
+BATCH = 8
 BATCHES = GROUPS // BATCH
+SOFT_STAGES = 4
 SCALE = D ** -0.5
 LAM_INIT = 0.8 - 0.6 * math.exp(-0.3 * 12)
 
@@ -66,20 +66,6 @@ def tile_differentialattention_pa_kernel(tc, x, Wq, Wk, lq1, lq2, lk1, lk2, out)
         vectors = const.tile([P, 4, D], BF16)
         for i, vec in enumerate((lq1, lq2, lk1, lk2)):
             nc.scalar.dma_start(out=vectors[:, i, :], in_=vec.partition_broadcast(P))
-        products = const.tile([P, 2, D], F32)
-        nc.vector.tensor_tensor(out=products[:], in0=vectors[:, 0:2, :], in1=vectors[:, 2:4, :], op=ALU.mult)
-        dots = const.tile([P, 2], F32)
-        nc.vector.tensor_reduce(out=dots[:], in_=products[:], axis=AXIS_X, op=ALU.add)
-        exps = const.tile([P, 2], F32)
-        nc.scalar.activation(out=exps[:], in_=dots[:], func=ACT.Exp)
-        neg_lam = const.tile([P, 1], F32)
-        nc.vector.tensor_scalar(
-            out=neg_lam[:], in0=exps[:, 1:2], scalar1=exps[:, 0:1], scalar2=-LAM_INIT, op0=ALU.subtract, op1=ALU.add
-        )
-        nc.vector.tensor_scalar(
-            out=select[:, 1, :], in0=select[:, 1, :], scalar1=neg_lam[:, 0:1], scalar2=None, op0=ALU.mult
-        )
-
         with tc.tile_pool(name="raw", bufs=3) as raw_pool, tc.tile_pool(name="grouped", bufs=2) as grouped_pool, tc.tile_pool(
             name="wq", bufs=2
         ) as w_pool, tc.tile_pool(name="xq", bufs=1) as x_pool, tc.tile_pool(name="y", bufs=2) as y_pool:
@@ -181,6 +167,13 @@ def tile_differentialattention_pa_kernel(tc, x, Wq, Wk, lq1, lq2, lk1, lk2, out)
             ready = {0: new_w_codes()}
             quantise(groupeds[0], ready[0][0], ready[0][1])
 
+            products = const.tile([P, 2, D], F32)
+            nc.vector.tensor_tensor(out=products[:], in0=vectors[:, 0:2, :], in1=vectors[:, 2:4, :], op=ALU.mult)
+            dots = const.tile([P, 2], F32)
+            nc.vector.tensor_reduce(out=dots[:], in_=products[:], axis=AXIS_X, op=ALU.add)
+            exps = const.tile([P, 2], F32)
+            nc.scalar.activation(out=exps[:], in_=dots[:], func=ACT.Exp)
+
             ys = {}
             for c in range(n_chunks):
                 if c + 2 < n_chunks:
@@ -197,54 +190,58 @@ def tile_differentialattention_pa_kernel(tc, x, Wq, Wk, lq1, lq2, lk1, lk2, out)
                 if c + 1 < n_chunks:
                     ready[c + 1] = new_w_codes()
                     quantise(groupeds[c + 1], ready[c + 1][0], ready[c + 1][1])
+            neg_lam = const.tile([P, 1], F32)
+            nc.vector.tensor_scalar(
+                out=neg_lam[:], in0=exps[:, 1:2], scalar1=exps[:, 0:1], scalar2=-LAM_INIT, op0=ALU.subtract, op1=ALU.add
+            )
+            nc.vector.tensor_scalar(
+                out=select[:, 1, :], in0=select[:, 1, :], scalar1=neg_lam[:, 0:1], scalar2=None, op0=ALU.mult
+            )
+
             for n in range(4):
                 turn_heads(ys[n_chunks - 1], n, True, HEADS_PER_CHUNK * (CHUNKS_PER_W - 1))
 
-        with tc.tile_pool(name="soft", bufs=4) as soft, tc.tile_pool(name="stats", bufs=4) as stats:
+        with tc.tile_pool(name="soft", bufs=SOFT_STAGES + 1) as soft, tc.tile_pool(name="stats", bufs=SOFT_STAGES + 1) as stats:
             wide = [P, BATCH, HEAD_ROWS]
             atts, tops, totals = {}, {}, {}
 
             def scores(b):
                 atts[b] = soft.tile(wide, F32, tag="att", name="att")
-                for half in range(BATCH // GROUPS_PER_BANK):
-                    bank = sums.tile([P, GROUPS_PER_BANK, 2 * HEAD_ROWS], F32, tag="sums")
-                    for i in range(GROUPS_PER_BANK):
-                        w = BATCH * b + GROUPS_PER_BANK * half + i
-                        nc.tensor.matmul(
-                            out=bank[:, i, :],
-                            lhsT=q_cols[:, 2 * w : 2 * w + 2, :].rearrange("p s c -> p (s c)"),
-                            rhs=k_cols[:, 2 * w : 2 * w + 2, :].rearrange("p s c -> p (s c)"),
-                            start=True,
-                            stop=True,
-                        )
-                    for u in range(2):
-                        rows = slice(D * u, D * u + D)
-                        nc.scalar.copy(
-                            out=atts[b][rows, GROUPS_PER_BANK * half : GROUPS_PER_BANK * (half + 1), :],
-                            in_=bank[rows, :, HEAD_ROWS * u : HEAD_ROWS * (u + 1)],
-                        )
+                bank = sums.tile([P, BATCH, 2 * HEAD_ROWS], F32, tag="sums")
+                for i in range(BATCH):
+                    w = BATCH * b + i
+                    nc.tensor.matmul(
+                        out=bank[:, i, :],
+                        lhsT=q_cols[:, 2 * w : 2 * w + 2, :].rearrange("p s c -> p (s c)"),
+                        rhs=k_cols[:, 2 * w : 2 * w + 2, :].rearrange("p s c -> p (s c)"),
+                        start=True,
+                        stop=True,
+                    )
+                for u in range(2):
+                    rows = slice(D * u, D * u + D)
+                    nc.scalar.copy(out=atts[b][rows], in_=bank[rows, :, HEAD_ROWS * u : HEAD_ROWS * (u + 1)])
 
             def largest(b):
                 tops[b] = stats.tile([P, BATCH], F32, tag="top", name="top")
                 nc.vector.tensor_reduce(out=tops[b][:], in_=atts[b][:], axis=AXIS_X, op=ALU.max)
 
-            def shift_and_exp(b):
-                att = atts[b]
+            def shift(b):
                 nc.vector.tensor_tensor(
-                    out=att[:], in0=att[:], in1=tops[b][:].unsqueeze(2).to_broadcast(wide), op=ALU.subtract
+                    out=atts[b][:], in0=atts[b][:], in1=tops[b][:].unsqueeze(2).to_broadcast(wide), op=ALU.subtract
                 )
-                nc.scalar.activation(out=att[:], in_=att[:], func=ACT.Exp, scale=SCALE)
+
+            def exponential(b):
+                nc.scalar.activation(out=atts[b][:], in_=atts[b][:], func=ACT.Exp, scale=SCALE)
 
             def add_up(b):
                 totals[b] = stats.tile([P, BATCH], F32, tag="total", name="total")
                 nc.vector.tensor_reduce(out=totals[b][:], in_=atts[b][:], axis=AXIS_X, op=ALU.add)
 
             def normalise(b):
-                att = atts[b]
                 inverse = stats.tile([P, BATCH], F32, tag="inverse")
                 nc.vector.reciprocal(out=inverse[:], in_=totals[b][:])
                 nc.vector.tensor_tensor(
-                    out=att[:], in0=att[:], in1=inverse[:].unsqueeze(2).to_broadcast(wide), op=ALU.mult
+                    out=atts[b][:], in0=atts[b][:], in1=inverse[:].unsqueeze(2).to_broadcast(wide), op=ALU.mult
                 )
 
             def combine(b):
@@ -257,15 +254,20 @@ def tile_differentialattention_pa_kernel(tc, x, Wq, Wk, lq1, lq2, lk1, lk2, out)
                 nc.scalar.copy(out=result[:], in_=diff[0 : 4 * H])
                 nc.sync.dma_start(out=out_rows[:, BATCH * b : BATCH * (b + 1), :], in_=result[:])
 
-            for b in range(BATCHES + 2):
-                if b < BATCHES:
+            def live(b):
+                return 0 <= b < BATCHES
+
+            for b in range(BATCHES + SOFT_STAGES - 1):
+                if live(b):
                     scores(b)
-                    largest(b)
-                if 1 <= b <= BATCHES:
-                    add_up(b - 1)
-                if b < BATCHES:
-                    shift_and_exp(b)
-                if 1 <= b <= BATCHES:
-                    normalise(b - 1)
-                if b >= 2:
-                    combine(b - 2)
+                if live(b - 1):
+                    largest(b - 1)
+                if live(b - 2):
+                    add_up(b - 2)
+                if live(b - 1):
+                    shift(b - 1)
+                    exponential(b - 1)
+                if live(b - 2):
+                    normalise(b - 2)
+                if live(b - 3):
+                    combine(b - 3)

@@ -31,7 +31,7 @@ SLOTS = TOKENS // 2
 GROUPS = SLOTS // 2
 BATCH = 8
 BATCHES = GROUPS // BATCH
-SOFT_STAGES = 4
+SOFT_STAGES = 7
 SCALE = D ** -0.5
 LAM_INIT = 0.8 - 0.6 * math.exp(-0.3 * 12)
 
@@ -42,7 +42,7 @@ def tile_differentialattention_pa_kernel(tc, x, Wq, Wk, lq1, lq2, lk1, lk2, out)
     nc = tc.nc
 
     x_rows = x.rearrange("b n c -> (b n) c").rearrange("(pr r t) c -> pr r t c", pr=2, t=2)
-    out_rows = out.rearrange("b n a h -> (b n a) h").rearrange("(w r) h -> r w h", r=4 * H)
+    out_rows = out.rearrange("b n a h -> (b n a) h").rearrange("(w u r) h -> u r w h", u=2, r=2 * H)
 
     with tc.manual_schedule(), tc.tile_pool(name="const", bufs=1) as const, tc.tile_pool(
         name="heads", bufs=1
@@ -55,13 +55,9 @@ def tile_differentialattention_pa_kernel(tc, x, Wq, Wk, lq1, lq2, lk1, lk2, out)
         for piece in range(16):
             nc.gpsimd.memset(q_cols[:, 16 * piece : 16 * piece + 16, :], 0.0)
 
-        select = const.tile([P, 2, P], F32)
-        nc.vector.memset(select[:], 0.0)
-        ident_rows = ident[:].rearrange("p (u j r) -> p u j r", u=2, j=2)
-        for j in range(2):
-            nc.vector.tensor_copy(
-                out=select[:, j, 0 : 4 * H].rearrange("p (u r) -> p u r", u=2), in_=ident_rows[:, :, j, :]
-            )
+        shift_up = const.tile([P, 2, 2, 2 * H], F32)
+        nc.vector.memset(shift_up[:], 0.0)
+        nc.vector.tensor_copy(out=shift_up[:, :, 0, :], in_=ident[:].rearrange("p (u j r) -> p u j r", u=2, j=2)[:, :, 1, :])
 
         vectors = const.tile([P, 4, D], BF16)
         for i, vec in enumerate((lq1, lq2, lk1, lk2)):
@@ -151,7 +147,8 @@ def tile_differentialattention_pa_kernel(tc, x, Wq, Wk, lq1, lq2, lk1, lk2, out)
             n_chunks = 2 * CHUNKS_PER_W
             x_raw = raw_pool.tile([P, ROW_TILES, C], BF16, tag="raw")
             for pr in range(2):
-                nc.sync.dma_start(out=x_raw[:, 2 * pr : 2 * pr + 2, :], in_=x_rows[pr])
+                for t in range(2):
+                    nc.sync.dma_start(out=x_raw[:, 2 * pr + t, :], in_=x_rows[pr][:, t, :])
             raws = {0: load_w(0), 1: load_w(1)}
 
             x_codes = x_pool.tile([P, PASSES, TOKENS], U32, align_bytes=64)
@@ -184,42 +181,42 @@ def tile_differentialattention_pa_kernel(tc, x, Wq, Wk, lq1, lq2, lk1, lk2, out)
                 for t in range(ROW_TILES):
                     if c + 1 < n_chunks:
                         turn_row_tile(raws[c + 1], groupeds[c + 1], t)
+                    if c + 1 < n_chunks and t == ROW_TILES - 1:
+                        ready[c + 1] = new_w_codes()
+                        quantise(groupeds[c + 1], ready[c + 1][0], ready[c + 1][1])
                     if c >= 1:
                         turn_heads(ys[c - 1], t, c - 1 >= CHUNKS_PER_W, HEADS_PER_CHUNK * ((c - 1) % CHUNKS_PER_W))
                     project_tile(ready[c][0], ready[c][1], ys[c], t)
-                if c + 1 < n_chunks:
-                    ready[c + 1] = new_w_codes()
-                    quantise(groupeds[c + 1], ready[c + 1][0], ready[c + 1][1])
             neg_lam = const.tile([P, 1], F32)
             nc.vector.tensor_scalar(
                 out=neg_lam[:], in0=exps[:, 1:2], scalar1=exps[:, 0:1], scalar2=-LAM_INIT, op0=ALU.subtract, op1=ALU.add
             )
-            nc.vector.tensor_scalar(
-                out=select[:, 1, :], in0=select[:, 1, :], scalar1=neg_lam[:, 0:1], scalar2=None, op0=ALU.mult
-            )
+            nc.vector.tensor_scalar(out=shift_up[:], in0=shift_up[:], scalar1=neg_lam[:, 0:1], scalar2=None, op0=ALU.mult)
 
             for n in range(4):
                 turn_heads(ys[n_chunks - 1], n, True, HEADS_PER_CHUNK * (CHUNKS_PER_W - 1))
 
         with tc.tile_pool(name="soft", bufs=SOFT_STAGES + 1) as soft, tc.tile_pool(name="stats", bufs=SOFT_STAGES + 1) as stats:
             wide = [P, BATCH, HEAD_ROWS]
-            atts, tops, totals = {}, {}, {}
+            banks, atts, tops, totals, inverses, moveds = {}, {}, {}, {}, {}, {}
 
             def scores(b):
-                atts[b] = soft.tile(wide, F32, tag="att", name="att")
-                bank = sums.tile([P, BATCH, 2 * HEAD_ROWS], F32, tag="sums")
+                banks[b] = sums.tile([P, BATCH, 2 * HEAD_ROWS], F32, tag="sums", name="bank")
                 for i in range(BATCH):
                     w = BATCH * b + i
                     nc.tensor.matmul(
-                        out=bank[:, i, :],
+                        out=banks[b][:, i, :],
                         lhsT=q_cols[:, 2 * w : 2 * w + 2, :].rearrange("p s c -> p (s c)"),
                         rhs=k_cols[:, 2 * w : 2 * w + 2, :].rearrange("p s c -> p (s c)"),
                         start=True,
                         stop=True,
                     )
+
+            def copy_scores(b):
+                atts[b] = soft.tile(wide, F32, tag="att", name="att")
                 for u in range(2):
                     rows = slice(D * u, D * u + D)
-                    nc.scalar.copy(out=atts[b][rows], in_=bank[rows, :, HEAD_ROWS * u : HEAD_ROWS * (u + 1)])
+                    nc.scalar.copy(out=atts[b][rows], in_=banks[b][rows, :, HEAD_ROWS * u : HEAD_ROWS * (u + 1)])
 
             def largest(b):
                 tops[b] = stats.tile([P, BATCH], F32, tag="top", name="top")
@@ -237,37 +234,54 @@ def tile_differentialattention_pa_kernel(tc, x, Wq, Wk, lq1, lq2, lk1, lk2, out)
                 totals[b] = stats.tile([P, BATCH], F32, tag="total", name="total")
                 nc.vector.tensor_reduce(out=totals[b][:], in_=atts[b][:], axis=AXIS_X, op=ALU.add)
 
-            def normalise(b):
-                inverse = stats.tile([P, BATCH], F32, tag="inverse")
-                nc.vector.reciprocal(out=inverse[:], in_=totals[b][:])
+            def invert(b):
+                inverses[b] = stats.tile([P, BATCH], F32, tag="inverse", name="inverse")
+                nc.vector.reciprocal(out=inverses[b][:], in_=totals[b][:])
+
+            def divide(b):
                 nc.vector.tensor_tensor(
-                    out=atts[b][:], in0=atts[b][:], in1=inverse[:].unsqueeze(2).to_broadcast(wide), op=ALU.mult
+                    out=atts[b][:], in0=atts[b][:], in1=inverses[b][:].unsqueeze(2).to_broadcast(wide), op=ALU.mult
                 )
 
-            def combine(b):
-                diff = turned.tile([P, BATCH, H], F32, tag="turned")
-                for j in range(2):
-                    nc.tensor.matmul(
-                        out=diff[:], lhsT=select[:, j, :], rhs=atts[b][:, :, H * j : H * j + H], start=(j == 0), stop=(j == 1)
+            def move_up(b):
+                moveds[b] = turned.tile([P, BATCH, H], F32, tag="turned", name="moved")
+                nc.tensor.matmul(
+                    out=moveds[b][:],
+                    lhsT=shift_up[:].rearrange("p u j r -> p (u j r)"),
+                    rhs=atts[b][:, :, H : 2 * H],
+                    start=True,
+                    stop=True,
+                )
+
+            def difference(b):
+                result = soft.tile([P, BATCH, H], F32, tag="result")
+                nc.vector.tensor_tensor(out=result[:], in0=atts[b][:, :, 0:H], in1=moveds[b][:], op=ALU.add)
+                for u in range(2):
+                    nc.sync.dma_start(
+                        out=out_rows[u][:, BATCH * b : BATCH * (b + 1), :], in_=result[D * u : D * u + 2 * H]
                     )
-                result = soft.tile([4 * H, BATCH, H], F32, tag="result")
-                nc.scalar.copy(out=result[:], in_=diff[0 : 4 * H])
-                nc.sync.dma_start(out=out_rows[:, BATCH * b : BATCH * (b + 1), :], in_=result[:])
 
             def live(b):
                 return 0 <= b < BATCHES
 
-            for b in range(BATCHES + SOFT_STAGES - 1):
-                if live(b):
-                    scores(b)
-                if live(b - 1):
-                    largest(b - 1)
-                if live(b - 2):
-                    add_up(b - 2)
-                if live(b - 1):
-                    shift(b - 1)
-                    exponential(b - 1)
-                if live(b - 2):
-                    normalise(b - 2)
-                if live(b - 3):
-                    combine(b - 3)
+            for r in range(BATCHES + SOFT_STAGES - 1):
+                if live(r):
+                    scores(r)
+                if live(r - 5):
+                    move_up(r - 5)
+                if live(r - 1):
+                    copy_scores(r - 1)
+                if live(r - 3):
+                    exponential(r - 3)
+                if live(r - 2):
+                    largest(r - 2)
+                if live(r - 4):
+                    add_up(r - 4)
+                if live(r - 2):
+                    shift(r - 2)
+                if live(r - 4):
+                    invert(r - 4)
+                if live(r - 6):
+                    difference(r - 6)
+                if live(r - 4):
+                    divide(r - 4)

import math

import concourse.mybir as mybir
from concourse.masks import make_identity

F32 = mybir.dt.float32
BF16 = mybir.dt.bfloat16
U32 = mybir.dt.uint32
U8 = mybir.dt.uint8
FP8X4 = mybir.dt.float8_e4m3fn_x4
ALU = mybir.AluOpType
ACT = mybir.ActivationFunctionType
AXIS_X = mybir.AxisListType.X

P = 128
PACK = 4
K_PASS = P * PACK
TOKENS = 512
C = 2048
DIM = 2048
H = 16
D = 64
HEAD_ROWS = 2 * H
PASSES = C // K_PASS
CHUNK = 512
ROW_TILES = CHUNK // P
CHUNKS_PER_W = DIM // CHUNK
HEADS_PER_CHUNK = CHUNK // (2 * D)
WORDS = P
SLOTS = TOKENS // 2
GROUPS = SLOTS // 2
BATCH = 8
BATCHES = GROUPS // BATCH
SOFT_STAGES = 7
SCALE = D ** -0.5
LAM_INIT = 0.8 - 0.6 * math.exp(-0.3 * 12)

FLOPS = 2 * TOKENS * C * DIM * 2 + 2 * TOKENS * HEAD_ROWS * HEAD_ROWS * D


def tile_differentialattention_pa_kernel(tc, x, Wq, Wk, lq1, lq2, lk1, lk2, out):
    nc = tc.nc

    x_rows = x.rearrange("b n c -> (b n) c").rearrange("(pr r t) c -> pr r t c", pr=2, t=2)
    out_rows = out.rearrange("b n a h -> (b n a) h").rearrange("(w u r) h -> u r w h", u=2, r=2 * H)

    with tc.manual_schedule(), tc.tile_pool(name="const", bufs=1) as const, tc.tile_pool(
        name="heads", bufs=1
    ) as heads, tc.psum_pool(name="turned", bufs=4) as turned, tc.psum_pool(name="sums", bufs=4) as sums:
        ident = const.tile([P, P], F32)
        make_identity(nc, ident[:])

        q_cols = heads.tile([P, SLOTS, 2 * HEAD_ROWS], F32)
        k_cols = heads.tile([P, SLOTS, HEAD_ROWS], F32)
        for piece in range(16):
            nc.gpsimd.memset(q_cols[:, 16 * piece : 16 * piece + 16, :], 0.0)

        shift_up = const.tile([P, 2, 2, 2 * H], F32)
        nc.vector.memset(shift_up[:], 0.0)
        nc.vector.tensor_copy(out=shift_up[:, :, 0, :], in_=ident[:].rearrange("p (u j r) -> p u j r", u=2, j=2)[:, :, 1, :])

        vectors = const.tile([P, 4, D], BF16)
        for i, vec in enumerate((lq1, lq2, lk1, lk2)):
            nc.scalar.dma_start(out=vectors[:, i, :], in_=vec.partition_broadcast(P))
        with tc.tile_pool(name="raw", bufs=3) as raw_pool, tc.tile_pool(name="grouped", bufs=2) as grouped_pool, tc.tile_pool(
            name="wq", bufs=2
        ) as w_pool, tc.tile_pool(name="xq", bufs=1) as x_pool, tc.tile_pool(name="y", bufs=2) as y_pool:

            def new_grouped():
                grouped = grouped_pool.tile([P, PASSES, PACK * CHUNK], BF16, align_bytes=64)
                return grouped

            def turn_row_tile(raw, grouped, r):
                raw_words = raw[:].bitcast(F32)
                grouped_words = grouped[:].bitcast(F32).rearrange("p g (o u) -> p g o u", u=2)
                for pair in range(PASSES // 2):
                    bank = turned.tile([P, 2, 2, P], F32, tag="turned")
                    for g in range(2):
                        for u in range(2):
                            first = 2 * WORDS * (2 * pair + g) + WORDS * u
                            nc.tensor.transpose(
                                out=bank[:, g, u, :], in_=raw_words[:, r, first : first + WORDS], identity=ident[:]
                            )
                    copy = nc.scalar.copy if pair == 0 else nc.vector.tensor_copy
                    copy(
                        out=grouped_words[:, 2 * pair : 2 * pair + 2, P * r : P * r + P, :],
                        in_=bank[:].rearrange("p g u o -> p g o u"),
                    )

            def quantise(grouped, codes, scales):
                for g in range(PASSES):
                    nc.vector.quantize_mx(
                        out=codes[:, g, :].bitcast(FP8X4), scales=scales[:, g, :], in_=grouped[:, g, :]
                    )

            def project_tile(w_codes, w_scales, y, t):
                tokens = slice(P * t, P * t + P)
                acc = sums.tile([P, CHUNK], F32, tag="sums")
                for g in range(PASSES):
                    nc.tensor.matmul_mx(
                        out=acc[:],
                        lhsT=x_codes[:, g, tokens].bitcast(FP8X4),
                        lhsT_scale=x_scales[:, g, tokens],
                        rhs=w_codes[:, g, :].bitcast(FP8X4),
                        rhs_scale=w_scales[:, g, :],
                        start=(g == 0),
                        stop=(g == PASSES - 1),
                    )
                nc.scalar.copy(
                    out=y[:, :, :, t, :], in_=acc[:].rearrange("p (h d j) -> p j h d", h=HEADS_PER_CHUNK, j=2)
                )

            def turn_heads(y, n, is_q, first_head):
                pr, j = n // 2, n % 2
                bank = turned.tile([P, HEADS_PER_CHUNK, P], F32, tag="turned")
                for h in range(HEADS_PER_CHUNK):
                    nc.tensor.transpose(
                        out=bank[:, h, :],
                        in_=y[:, j, h, 2 * pr : 2 * pr + 2, :].rearrange("p t d -> p (t d)"),
                        identity=ident[:],
                    )
                by_slot = bank[:].rearrange("p h s -> p s h")
                slots = slice(P * pr, P * pr + P)
                copy = nc.vector.tensor_copy if n % 2 == 0 else nc.scalar.copy
                if is_q:
                    for t in range(2):
                        rows = slice(D * t, D * t + D)
                        col = 2 * H * j + H * t + first_head
                        copy(out=q_cols[rows, slots, col : col + HEADS_PER_CHUNK], in_=by_slot[rows])
                else:
                    col = H * j + first_head
                    copy(out=k_cols[:, slots, col : col + HEADS_PER_CHUNK], in_=by_slot)

            def load_w(c):
                w = Wk if c < CHUNKS_PER_W else Wq
                first = CHUNK * (c % CHUNKS_PER_W)
                raw = raw_pool.tile([P, ROW_TILES, C], BF16, tag="raw")
                for r in range(ROW_TILES):
                    nc.sync.dma_start(out=raw[:, r, :], in_=w[first + P * r : first + P * r + P, :])
                return raw

            def new_w_codes():
                codes = w_pool.tile([P, PASSES, CHUNK], U32, align_bytes=64, tag="w_codes")
                scales = w_pool.tile([P, PASSES, CHUNK], U8, align_bytes=64, tag="w_scales")
                return codes, scales

            n_chunks = 2 * CHUNKS_PER_W
            x_raw = raw_pool.tile([P, ROW_TILES, C], BF16, tag="raw")
            for pr in range(2):
                for t in range(2):
                    nc.sync.dma_start(out=x_raw[:, 2 * pr + t, :], in_=x_rows[pr][:, t, :])
            raws = {0: load_w(0), 1: load_w(1)}

            x_codes = x_pool.tile([P, PASSES, TOKENS], U32, align_bytes=64)
            x_scales = x_pool.tile([P, PASSES, TOKENS], U8, align_bytes=64)
            x_grouped = new_grouped()
            for r in range(ROW_TILES):
                turn_row_tile(x_raw, x_grouped, r)
            quantise(x_grouped, x_codes, x_scales)

            groupeds = {0: new_grouped()}
            for r in range(ROW_TILES):
                turn_row_tile(raws[0], groupeds[0], r)
            ready = {0: new_w_codes()}
            quantise(groupeds[0], ready[0][0], ready[0][1])

            products = const.tile([P, 2, D], F32)
            nc.vector.tensor_tensor(out=products[:], in0=vectors[:, 0:2, :], in1=vectors[:, 2:4, :], op=ALU.mult)
            dots = const.tile([P, 2], F32)
            nc.vector.tensor_reduce(out=dots[:], in_=products[:], axis=AXIS_X, op=ALU.add)
            exps = const.tile([P, 2], F32)
            nc.scalar.activation(out=exps[:], in_=dots[:], func=ACT.Exp)

            ys = {}
            for c in range(n_chunks):
                if c + 2 < n_chunks:
                    raws[c + 2] = load_w(c + 2)
                if c + 1 < n_chunks:
                    groupeds[c + 1] = new_grouped()
                ys[c] = y_pool.tile([P, 2, HEADS_PER_CHUNK, ROW_TILES, D], F32, tag="y", name="y")
                for t in range(ROW_TILES):
                    if c + 1 < n_chunks:
                        turn_row_tile(raws[c + 1], groupeds[c + 1], t)
                    if c + 1 < n_chunks and t == ROW_TILES - 1:
                        ready[c + 1] = new_w_codes()
                        quantise(groupeds[c + 1], ready[c + 1][0], ready[c + 1][1])
                    if c >= 1:
                        turn_heads(ys[c - 1], t, c - 1 >= CHUNKS_PER_W, HEADS_PER_CHUNK * ((c - 1) % CHUNKS_PER_W))
                    project_tile(ready[c][0], ready[c][1], ys[c], t)
            neg_lam = const.tile([P, 1], F32)
            nc.vector.tensor_scalar(
                out=neg_lam[:], in0=exps[:, 1:2], scalar1=exps[:, 0:1], scalar2=-LAM_INIT, op0=ALU.subtract, op1=ALU.add
            )
            nc.vector.tensor_scalar(out=shift_up[:], in0=shift_up[:], scalar1=neg_lam[:, 0:1], scalar2=None, op0=ALU.mult)

            for n in range(4):
                turn_heads(ys[n_chunks - 1], n, True, HEADS_PER_CHUNK * (CHUNKS_PER_W - 1))

        with tc.tile_pool(name="soft", bufs=SOFT_STAGES + 1) as soft, tc.tile_pool(name="stats", bufs=SOFT_STAGES + 1) as stats:
            wide = [P, BATCH, HEAD_ROWS]
            banks, atts, tops, totals, inverses, moveds = {}, {}, {}, {}, {}, {}

            def scores(b):
                banks[b] = sums.tile([P, BATCH, 2 * HEAD_ROWS], F32, tag="sums", name="bank")
                for i in range(BATCH):
                    w = BATCH * b + i
                    nc.tensor.matmul(
                        out=banks[b][:, i, :],
                        lhsT=q_cols[:, 2 * w : 2 * w + 2, :].rearrange("p s c -> p (s c)"),
                        rhs=k_cols[:, 2 * w : 2 * w + 2, :].rearrange("p s c -> p (s c)"),
                        start=True,
                        stop=True,
                    )

            def copy_scores(b):
                atts[b] = soft.tile(wide, F32, tag="att", name="att")
                for u in range(2):
                    rows = slice(D * u, D * u + D)
                    nc.scalar.copy(out=atts[b][rows], in_=banks[b][rows, :, HEAD_ROWS * u : HEAD_ROWS * (u + 1)])

            def largest(b):
                tops[b] = stats.tile([P, BATCH], F32, tag="top", name="top")
                nc.vector.tensor_reduce(out=tops[b][:], in_=atts[b][:], axis=AXIS_X, op=ALU.max)

            def shift(b):
                nc.vector.tensor_tensor(
                    out=atts[b][:], in0=atts[b][:], in1=tops[b][:].unsqueeze(2).to_broadcast(wide), op=ALU.subtract
                )

            def exponential(b):
                nc.scalar.activation(out=atts[b][:], in_=atts[b][:], func=ACT.Exp, scale=SCALE)

            def add_up(b):
                totals[b] = stats.tile([P, BATCH], F32, tag="total", name="total")
                nc.vector.tensor_reduce(out=totals[b][:], in_=atts[b][:], axis=AXIS_X, op=ALU.add)

            def invert(b):
                inverses[b] = stats.tile([P, BATCH], F32, tag="inverse", name="inverse")
                nc.vector.reciprocal(out=inverses[b][:], in_=totals[b][:])

            def divide(b):
                nc.vector.tensor_tensor(
                    out=atts[b][:], in0=atts[b][:], in1=inverses[b][:].unsqueeze(2).to_broadcast(wide), op=ALU.mult
                )

            def move_up(b):
                moveds[b] = turned.tile([P, BATCH, H], F32, tag="turned", name="moved")
                nc.tensor.matmul(
                    out=moveds[b][:],
                    lhsT=shift_up[:].rearrange("p u j r -> p (u j r)"),
                    rhs=atts[b][:, :, H : 2 * H],
                    start=True,
                    stop=True,
                )

            def difference(b):
                result = soft.tile([P, BATCH, H], F32, tag="result")
                nc.vector.tensor_tensor(out=result[:], in0=atts[b][:, :, 0:H], in1=moveds[b][:], op=ALU.add)
                for u in range(2):
                    nc.sync.dma_start(
                        out=out_rows[u][:, BATCH * b : BATCH * (b + 1), :], in_=result[D * u : D * u + 2 * H]
                    )

            def live(b):
                return 0 <= b < BATCHES

            for r in range(BATCHES + SOFT_STAGES - 1):
                if live(r):
                    scores(r)
                if live(r - 5):
                    move_up(r - 5)
                if live(r - 1):
                    copy_scores(r - 1)
                if live(r - 3):
                    exponential(r - 3)
                if live(r - 2):
                    largest(r - 2)
                if live(r - 4):
                    add_up(r - 4)
                if live(r - 2):
                    shift(r - 2)
                if live(r - 4):
                    invert(r - 4)
                if live(r - 6):
                    difference(r - 6)
                if live(r - 4):
                    divide(r - 4)
